import numpy as np
import ml_dtypes


def mxq(x, axis, fmt="e4m3"):
    dtype, down = {"e4m3": (ml_dtypes.float8_e4m3fn, 7), "e5m2": (ml_dtypes.float8_e5m2, 14)}[fmt]
    v = np.moveaxis(np.asarray(x, np.float32).astype(ml_dtypes.bfloat16).astype(np.float64), axis, -1)
    blocks = v.reshape(v.shape[:-1] + (-1, 32))
    amax = np.abs(blocks).max(-1, keepdims=True)
    byte = np.maximum(np.where(amax > 0, np.frexp(amax)[1] - 1 + 127, 0) - down, 1)
    scale = np.exp2(byte - 127.0)
    codes = (blocks / scale).astype(np.float32).astype(dtype).astype(np.float64)
    return np.moveaxis((codes * scale).reshape(v.shape), -1, axis)


WIDE = False


def mx_kscale(k):
    if not WIDE:
        return np.ones(k)
    levels = np.array([10, -10, 5, -5, 0])
    a = np.random.permutation(np.resize(levels, k // 512 * 4)).reshape(k // 512, 4)
    idx = np.arange(k)
    return np.exp2(a[idx // 512, idx % 128 // 32])


BF16 = ml_dtypes.bfloat16


def bf(x):
    return np.asarray(x, np.float32).astype(BF16)


def f64(x):
    return np.asarray(x).astype(np.float64)


E2M1 = np.array([0.0, 0.5, 1.0, 1.5, 2.0, 3.0, 4.0, 6.0, -0.0, -0.5, -1.0, -1.5, -2.0, -3.0, -4.0, -6.0])


def pack_weight(w, fmt):
    k, n = w.shape
    w = f64(bf(w)).reshape(k // 32, 32, n)
    amax = np.abs(w).max(1)
    if fmt == "e4m3":
        byte = np.frexp(amax)[1] - 1 + 127 - 7
    else:
        mant, ex = np.frexp(amax / 6.0)
        byte = np.where(mant > 0.5, ex, ex - 1) + 127
    byte = np.clip(np.where(amax > 0, byte, 1), 1, 254)
    scaled = (w * np.exp2(127.0 - byte)[:, None, :]).reshape(k, n).astype(np.float32)
    by_word = np.ascontiguousarray(scaled.reshape(k // 512, 128, 4, n).transpose(0, 1, 3, 2))
    if fmt == "e4m3":
        words = by_word.astype(ml_dtypes.float8_e4m3fn).view(np.uint8)
    else:
        c = by_word.astype(ml_dtypes.float4_e2m1fn).view(np.uint8) & 0xF
        words = c[..., 0::2] | (c[..., 1::2] << 4)
    return np.ascontiguousarray(words), np.ascontiguousarray(byte.astype(np.uint8).reshape(k // 512, 16, n))


def unpack_weight(words, scales, fmt):
    g, p, n, _ = words.shape
    if fmt == "e4m3":
        vals = np.ascontiguousarray(words).view(ml_dtypes.float8_e4m3fn).astype(np.float64)
    else:
        nib = np.empty((g, p, n, 4), np.uint8)
        nib[..., 0::2] = words & 0xF
        nib[..., 1::2] = words >> 4
        vals = E2M1[nib]
    vals = vals * np.repeat(np.exp2(scales.astype(np.float64) - 127.0), 8, axis=1)[..., None]
    return vals.transpose(0, 1, 3, 2).reshape(g * 512, n)

def pack4(w):
    words, scales = pack_weight(w, "e2m1")
    return words.reshape(words.shape[0], 128, -1), scales


def unpack4(words, scales):
    return unpack_weight(words.reshape(words.shape[0], 128, -1, 2), scales, "e2m1")


B, S, D, NH, NKV, HD = 1, 128, 512, 16, 4, 128
ROPE_THETA = 10000.0


def rope_tables():
    freqs = 1.0 / (ROPE_THETA ** (f64(np.arange(0, HD, 2)) / HD))
    ang = np.outer(f64(np.arange(S)), freqs)
    return np.cos(ang), np.sin(ang)


def rope(x, cos, sin):
    xr = x.reshape(*x.shape[:-1], HD // 2, 2)
    re, im = xr[..., 0], xr[..., 1]
    c = cos[None, :, None, :]
    s = sin[None, :, None, :]
    return np.stack((re * c - im * s, re * s + im * c), axis=-1).reshape(x.shape)


def setup_inputs():
    s = mx_kscale(D)
    hidden_states = bf(np.random.standard_normal((B, S, D)) * s)
    wq_words, wq_scales = pack4(np.random.standard_normal((D, NH * HD)) / np.sqrt(D) / s[:, None])
    wk_words, wk_scales = pack4(np.random.standard_normal((D, NKV * HD)) / np.sqrt(D) / s[:, None])
    wv_words, wv_scales = pack4(np.random.standard_normal((D, NKV * HD)) * 2.0 / np.sqrt(D) / s[:, None])
    return {"hidden_states": hidden_states,
            "wq_words": wq_words, "wq_scales": wq_scales,
            "wk_words": wk_words, "wk_scales": wk_scales,
            "wv_words": wv_words, "wv_scales": wv_scales}


def reference(hidden_states, wq_words, wq_scales, wk_words, wk_scales, wv_words, wv_scales):
    xq = mxq(f64(hidden_states), 2, "e4m3")
    q = (xq @ unpack4(wq_words, wq_scales)).reshape(B, S, NH, HD)
    k = (xq @ unpack4(wk_words, wk_scales)).reshape(B, S, NKV, HD)
    v = (xq @ unpack4(wv_words, wv_scales)).reshape(B, S, NKV, HD)
    cos, sin = rope_tables()
    return rope(q, cos, sin), rope(k, cos, sin), v

@@ -1,0 +1,185 @@
+import math
+from contextlib import ExitStack
+
+import concourse.mybir as mybir
+from concourse.masks import make_identity
+
+F32 = mybir.dt.float32
+BF16 = mybir.dt.bfloat16
+I32 = mybir.dt.int32
+U32 = mybir.dt.uint32
+U8 = mybir.dt.uint8
+FP8X4 = mybir.dt.float8_e4m3fn_x4
+FP4X4 = mybir.dt.float4_e2m1fn_x4
+ALU = mybir.AluOpType
+ACT = mybir.ActivationFunctionType
+
+P = 128
+TOKENS = 128
+D_MODEL = 512
+HEAD_DIM = 128
+PAIRS = HEAD_DIM // 2
+Q_HEADS = 16
+KV_HEADS = 4
+ROPE_THETA = 10000.0
+BANK_COLS = 512
+BANK_HEADS = BANK_COLS // HEAD_DIM
+N_BANKS = (Q_HEADS + 2 * KV_HEADS) // BANK_HEADS
+QUADRANT = 32
+LIVE_ROWS = 4
+ROUND_MAGIC = 1.5 * 2.0**23
+NEG_SIN = 0
+SIN = 1
+COS = 2
+
+FLOPS = 2 * TOKENS * D_MODEL * (Q_HEADS + 2 * KV_HEADS) * HEAD_DIM
+
+
+def load_weight(nc, pool, words, scales, name):
+    n_cols = scales.shape[2]
+    words_sb = pool.tile([P, 2 * n_cols], U8, name=name + "_words", align_bytes=64)
+    nc.sync.dma_start(out=words_sb[:].bitcast(I32), in_=words.bitcast(I32)[0])
+
+    plane = pool.tile([P, n_cols], U8, name=name + "_plane", align_bytes=64)
+    nc.vector.memset(plane[:].bitcast(I32), 0)
+    rows = scales.bitcast(I32)[0].rearrange("(q r) n -> r q n", r=LIVE_ROWS)
+    for r in range(LIVE_ROWS):
+        nc.sync.dma_start(out=plane[:].bitcast(I32)[r:P:QUADRANT, :], in_=rows[r])
+    return words_sb, plane
+
+
+def quantise_activations(nc, pool, psum, x_sb):
+    ident = pool.tile([P, P], F32)
+    make_identity(nc, ident[:])
+    x_pairs = x_sb[:].bitcast(F32)
+    halves = psum.tile([P, 2, TOKENS], F32)
+    for u in range(2):
+        nc.tensor.transpose(out=halves[:, u, :], in_=x_pairs[:, u : D_MODEL // 2 : 2], identity=ident[:])
+    grouped = pool.tile([P, 4 * TOKENS], BF16, align_bytes=64)
+    nc.scalar.copy(
+        out=grouped[:].bitcast(F32).rearrange("p (r u) -> p r u", u=2),
+        in_=halves[:].rearrange("p u r -> p r u"),
+    )
+    codes = pool.tile([P, TOKENS], U32, align_bytes=64)
+    scales = pool.tile([P, TOKENS], U8, align_bytes=64)
+    nc.vector.quantize_mx(out=codes[:].bitcast(FP8X4), scales=scales[:], in_=grouped[:])
+    return codes, scales
+
+
+def rotary_table(nc, pool):
+    warm = pool.tile([P, 1], F32)
+    nc.gpsimd.memset(warm[:], 0.0)
+    warmed = pool.tile([P, 1], F32)
+    nc.scalar.activation(out=warmed[:], in_=warm[:], func=ACT.Sin)
+
+    position = pool.tile([P, 1], F32)
+    nc.gpsimd.iota(
+        position[:], pattern=[[0, 1]], base=0, channel_multiplier=1, allow_small_or_imprecise_dtypes=True
+    )
+    turns = pool.tile([P, 1], F32)
+    nc.vector.tensor_scalar_mul(out=turns[:], in0=position[:], scalar1=1.0 / (2.0 * math.pi))
+
+    ratio = ROPE_THETA ** (-2.0 / HEAD_DIM)
+    freq = pool.tile([P, PAIRS], F32)
+    nc.vector.memset(freq[:, 0:1], 1.0)
+    width = 1
+    while width < PAIRS:
+        nc.vector.tensor_scalar_mul(
+            out=freq[:, width : 2 * width], in0=freq[:, 0:width], scalar1=ratio**width
+        )
+        width *= 2
+
+    angle = pool.tile([P, 2, PAIRS], F32)
+    for i, lead in enumerate((0.0, 0.25)):
+        nc.vector.tensor_scalar(
+            out=angle[:, i, :], in0=freq[:], scalar1=turns[:, 0:1], scalar2=lead, op0=ALU.mult, op1=ALU.add
+        )
+    whole = pool.tile([P, 2, PAIRS], F32)
+    nc.vector.tensor_scalar(
+        out=whole[:], in0=angle[:], scalar1=ROUND_MAGIC, scalar2=ROUND_MAGIC, op0=ALU.add, op1=ALU.subtract
+    )
+    part = pool.tile([P, 2, PAIRS], F32)
+    nc.vector.tensor_tensor(out=part[:], in0=angle[:], in1=whole[:], op=ALU.subtract)
+
+    table = pool.tile([P, 3, PAIRS], F32)
+    nc.scalar.activation(out=table[:, SIN : COS + 1, :], in_=part[:], func=ACT.Sin, scale=2.0 * math.pi)
+    nc.scalar.activation(out=table[:, NEG_SIN, :], in_=part[:, 0, :], func=ACT.Sin, scale=-2.0 * math.pi)
+    return table
+
+
+def rotate_bank(nc, pool, acc, table, rotated, adder):
+    pairs = "p (h j e) -> p h j e"
+    acc_pairs = acc[:].rearrange(pairs, h=BANK_HEADS, e=2)
+    own = pool.tile([TOKENS, BANK_COLS], F32)
+    nc.vector.tensor_tensor(
+        out=own[:].rearrange(pairs, h=BANK_HEADS, e=2),
+        in0=acc_pairs,
+        in1=table[:, COS : COS + 1, :].unsqueeze(3).to_broadcast([TOKENS, BANK_HEADS, PAIRS, 2]),
+        op=ALU.mult,
+    )
+    partner = pool.tile([TOKENS, 2, BANK_HEADS, PAIRS], F32)
+    for e, sine in enumerate((NEG_SIN, SIN)):
+        nc.vector.tensor_tensor(
+            out=partner[:, e],
+            in0=acc_pairs[:, :, :, 1 - e],
+            in1=table[:, sine : sine + 1, :].to_broadcast([TOKENS, BANK_HEADS, PAIRS]),
+            op=ALU.mult,
+        )
+    adder.tensor_tensor(
+        out=rotated[:].rearrange(pairs, h=BANK_HEADS, e=2),
+        in0=own[:].rearrange(pairs, h=BANK_HEADS, e=2),
+        in1=partner[:].rearrange("p e h j -> p h j e"),
+        op=ALU.add,
+    )
+
+
+def tile_rptattention_pa_s_kernel(
+    tc, hidden_states, wq_words, wq_scales, wk_words, wk_scales, wv_words, wv_scales, out_0, out_1, out_2
+):
+    nc = tc.nc
+    with ExitStack() as ctx:
+        keep = ctx.enter_context(tc.tile_pool(name="keep", bufs=1))
+        work = ctx.enter_context(tc.tile_pool(name="work", bufs=N_BANKS))
+        psum_x = ctx.enter_context(tc.psum_pool(name="psum_x", bufs=1))
+        psum_acc = ctx.enter_context(tc.psum_pool(name="psum_acc", bufs=N_BANKS))
+
+        x_sb = keep.tile([TOKENS, D_MODEL], BF16)
+        nc.sync.dma_start(out=x_sb[:], in_=hidden_states.rearrange("b s d -> (b s) d"))
+        wk = load_weight(nc, keep, wk_words, wk_scales, "wk")
+        wq = load_weight(nc, keep, wq_words, wq_scales, "wq")
+        wv = load_weight(nc, keep, wv_words, wv_scales, "wv")
+
+        table = rotary_table(nc, keep)
+        x_codes, x_scales = quantise_activations(nc, keep, psum_x, x_sb)
+
+        def project(weight, b):
+            words_sb, plane = weight
+            acc = psum_acc.tile([TOKENS, BANK_COLS], F32)
+            nc.tensor.matmul_mx(
+                out=acc[:],
+                lhsT=x_codes[:].bitcast(FP8X4),
+                lhsT_scale=x_scales[:],
+                rhs=words_sb[:, 2 * b * BANK_COLS : 2 * (b + 1) * BANK_COLS].bitcast(FP4X4),
+                rhs_scale=plane[:, b * BANK_COLS : (b + 1) * BANK_COLS],
+                start=True,
+                stop=True,
+            )
+            return acc
+
+        flat = "b s h d -> (b s) (h d)"
+        q_rot = out_0.rearrange(flat)
+        rotated_banks = [(wk, 0, out_1.rearrange(flat))]
+        for b in range(Q_HEADS // BANK_HEADS):
+            rotated_banks.append((wq, b, q_rot[:, b * BANK_COLS : (b + 1) * BANK_COLS]))
+
+        for i, (weight, b, dest) in enumerate(rotated_banks):
+            acc = project(weight, b)
+            rotated = work.tile([TOKENS, BANK_COLS], F32)
+            is_last = i == len(rotated_banks) - 1
+            rotate_bank(nc, work, acc, table, rotated, nc.vector if is_last else nc.gpsimd)
+            nc.sync.dma_start(out=dest, in_=rotated[:])
+
+        acc = project(wv, 0)
+        v_sb = keep.tile([TOKENS, BANK_COLS], F32)
+        nc.scalar.copy(out=v_sb[:], in_=acc[:])
+        nc.sync.dma_start(out=out_2.rearrange(flat), in_=v_sb[:])

@@ -28,9 +28,10 @@ N_BANKS = (Q_HEADS + 2 * KV_HEADS) // BANK_HEADS
 QUADRANT = 32
 LIVE_ROWS = 4
 ROUND_MAGIC = 1.5 * 2.0**23
-NEG_SIN = 0
+COS = 0
 SIN = 1
-COS = 2
+
+VECTOR_ADDS = 2
 
 FLOPS = 2 * TOKENS * D_MODEL * (Q_HEADS + 2 * KV_HEADS) * HEAD_DIM
 
@@ -101,34 +102,37 @@ def rotary_table(nc, pool):
     part = pool.tile([P, 2, PAIRS], F32)
     nc.vector.tensor_tensor(out=part[:], in0=angle[:], in1=whole[:], op=ALU.subtract)
 
-    table = pool.tile([P, 3, PAIRS], F32)
-    nc.scalar.activation(out=table[:, SIN : COS + 1, :], in_=part[:], func=ACT.Sin, scale=2.0 * math.pi)
-    nc.scalar.activation(out=table[:, NEG_SIN, :], in_=part[:, 0, :], func=ACT.Sin, scale=-2.0 * math.pi)
+    table = pool.tile([P, 2, HEAD_DIM], F32)
+    by_pair = table[:].rearrange("p c (j e) -> p c j e", e=2)
+    nc.scalar.activation(
+        out=by_pair[:, COS],
+        in_=part[:, 1, :].unsqueeze(2).to_broadcast([P, PAIRS, 2]),
+        func=ACT.Sin,
+        scale=2.0 * math.pi,
+    )
+    nc.scalar.activation(out=by_pair[:, SIN, :, 0], in_=part[:, 0, :], func=ACT.Sin, scale=2.0 * math.pi)
+    nc.scalar.activation(out=by_pair[:, SIN, :, 1], in_=part[:, 0, :], func=ACT.Sin, scale=-2.0 * math.pi)
     return table
 
 
-def rotate_bank(nc, pool, acc, table, rotated, adder):
-    pairs = "p (h j e) -> p h j e"
-    acc_pairs = acc[:].rearrange(pairs, h=BANK_HEADS, e=2)
-    own = pool.tile([TOKENS, BANK_COLS], F32)
+def multiply_bank(nc, pool, acc, table):
+    shape = [TOKENS, 2, BANK_HEADS, HEAD_DIM]
+    products = pool.tile(shape, F32)
     nc.vector.tensor_tensor(
-        out=own[:].rearrange(pairs, h=BANK_HEADS, e=2),
-        in0=acc_pairs,
-        in1=table[:, COS : COS + 1, :].unsqueeze(3).to_broadcast([TOKENS, BANK_HEADS, PAIRS, 2]),
+        out=products[:],
+        in0=acc[:].rearrange("p (h d) -> p h d", h=BANK_HEADS).unsqueeze(1).to_broadcast(shape),
+        in1=table[:].unsqueeze(2).to_broadcast(shape),
         op=ALU.mult,
     )
-    partner = pool.tile([TOKENS, 2, BANK_HEADS, PAIRS], F32)
-    for e, sine in enumerate((NEG_SIN, SIN)):
-        nc.vector.tensor_tensor(
-            out=partner[:, e],
-            in0=acc_pairs[:, :, :, 1 - e],
-            in1=table[:, sine : sine + 1, :].to_broadcast([TOKENS, BANK_HEADS, PAIRS]),
-            op=ALU.mult,
-        )
+    return products
+
+
+def add_bank(adder, products, rotated):
+    pairs = "p h (j e) -> p (h j) e"
     adder.tensor_tensor(
-        out=rotated[:].rearrange(pairs, h=BANK_HEADS, e=2),
-        in0=own[:].rearrange(pairs, h=BANK_HEADS, e=2),
-        in1=partner[:].rearrange("p e h j -> p h j e"),
+        out=rotated[:].rearrange("p (n e) -> p n e", e=2),
+        in0=products[:, COS].rearrange(pairs, e=2),
+        in1=products[:, SIN].rearrange(pairs, e=2)[:, :, ::-1],
         op=ALU.add,
     )
 
@@ -172,11 +176,19 @@ def tile_rptattention_pa_s_kernel(
         for b in range(Q_HEADS // BANK_HEADS):
             rotated_banks.append((wq, b, q_rot[:, b * BANK_COLS : (b + 1) * BANK_COLS]))
 
+        waiting = []
         for i, (weight, b, dest) in enumerate(rotated_banks):
             acc = project(weight, b)
+            products = multiply_bank(nc, work, acc, table)
+            if i < len(rotated_banks) - VECTOR_ADDS:
+                rotated = work.tile([TOKENS, BANK_COLS], F32)
+                add_bank(nc.gpsimd, products, rotated)
+                nc.sync.dma_start(out=dest, in_=rotated[:])
+            else:
+                waiting.append((products, dest))
+        for products, dest in waiting:
             rotated = work.tile([TOKENS, BANK_COLS], F32)
-            is_last = i == len(rotated_banks) - 1
-            rotate_bank(nc, work, acc, table, rotated, nc.vector if is_last else nc.gpsimd)
+            add_bank(nc.vector, products, rotated)
             nc.sync.dma_start(out=dest, in_=rotated[:])
 
         acc = project(wv, 0)

@@ -24,95 +24,29 @@ KV_HEADS = 4
 ROPE_THETA = 10000.0
 BANK_COLS = 512
 BANK_HEADS = BANK_COLS // HEAD_DIM
+Q_BANKS = Q_HEADS // BANK_HEADS
 N_BANKS = (Q_HEADS + 2 * KV_HEADS) // BANK_HEADS
 QUADRANT = 32
 LIVE_ROWS = 4
 ROUND_MAGIC = 1.5 * 2.0**23
 COS = 0
 SIN = 1
-
 VECTOR_ADDS = 2
+FINE = 8
 
 FLOPS = 2 * TOKENS * D_MODEL * (Q_HEADS + 2 * KV_HEADS) * HEAD_DIM
 
 
-def load_weight(nc, pool, words, scales, name):
-    n_cols = scales.shape[2]
-    words_sb = pool.tile([P, 2 * n_cols], U8, name=name + "_words", align_bytes=64)
+def load_words(nc, pool, words, name):
+    words_sb = pool.tile([P, words.shape[2]], U8, name=name, align_bytes=64)
     nc.sync.dma_start(out=words_sb[:].bitcast(I32), in_=words.bitcast(I32)[0])
+    return words_sb
 
-    plane = pool.tile([P, n_cols], U8, name=name + "_plane", align_bytes=64)
-    nc.vector.memset(plane[:].bitcast(I32), 0)
+
+def load_scales(nc, plane, scales):
     rows = scales.bitcast(I32)[0].rearrange("(q r) n -> r q n", r=LIVE_ROWS)
     for r in range(LIVE_ROWS):
-        nc.sync.dma_start(out=plane[:].bitcast(I32)[r:P:QUADRANT, :], in_=rows[r])
-    return words_sb, plane
-
-
-def quantise_activations(nc, pool, psum, x_sb):
-    ident = pool.tile([P, P], F32)
-    make_identity(nc, ident[:])
-    x_pairs = x_sb[:].bitcast(F32)
-    halves = psum.tile([P, 2, TOKENS], F32)
-    for u in range(2):
-        nc.tensor.transpose(out=halves[:, u, :], in_=x_pairs[:, u : D_MODEL // 2 : 2], identity=ident[:])
-    grouped = pool.tile([P, 4 * TOKENS], BF16, align_bytes=64)
-    nc.scalar.copy(
-        out=grouped[:].bitcast(F32).rearrange("p (r u) -> p r u", u=2),
-        in_=halves[:].rearrange("p u r -> p r u"),
-    )
-    codes = pool.tile([P, TOKENS], U32, align_bytes=64)
-    scales = pool.tile([P, TOKENS], U8, align_bytes=64)
-    nc.vector.quantize_mx(out=codes[:].bitcast(FP8X4), scales=scales[:], in_=grouped[:])
-    return codes, scales
-
-
-def rotary_table(nc, pool):
-    warm = pool.tile([P, 1], F32)
-    nc.gpsimd.memset(warm[:], 0.0)
-    warmed = pool.tile([P, 1], F32)
-    nc.scalar.activation(out=warmed[:], in_=warm[:], func=ACT.Sin)
-
-    position = pool.tile([P, 1], F32)
-    nc.gpsimd.iota(
-        position[:], pattern=[[0, 1]], base=0, channel_multiplier=1, allow_small_or_imprecise_dtypes=True
-    )
-    turns = pool.tile([P, 1], F32)
-    nc.vector.tensor_scalar_mul(out=turns[:], in0=position[:], scalar1=1.0 / (2.0 * math.pi))
-
-    ratio = ROPE_THETA ** (-2.0 / HEAD_DIM)
-    freq = pool.tile([P, PAIRS], F32)
-    nc.vector.memset(freq[:, 0:1], 1.0)
-    width = 1
-    while width < PAIRS:
-        nc.vector.tensor_scalar_mul(
-            out=freq[:, width : 2 * width], in0=freq[:, 0:width], scalar1=ratio**width
-        )
-        width *= 2
-
-    angle = pool.tile([P, 2, PAIRS], F32)
-    for i, lead in enumerate((0.0, 0.25)):
-        nc.vector.tensor_scalar(
-            out=angle[:, i, :], in0=freq[:], scalar1=turns[:, 0:1], scalar2=lead, op0=ALU.mult, op1=ALU.add
-        )
-    whole = pool.tile([P, 2, PAIRS], F32)
-    nc.vector.tensor_scalar(
-        out=whole[:], in0=angle[:], scalar1=ROUND_MAGIC, scalar2=ROUND_MAGIC, op0=ALU.add, op1=ALU.subtract
-    )
-    part = pool.tile([P, 2, PAIRS], F32)
-    nc.vector.tensor_tensor(out=part[:], in0=angle[:], in1=whole[:], op=ALU.subtract)
-
-    table = pool.tile([P, 2, HEAD_DIM], F32)
-    by_pair = table[:].rearrange("p c (j e) -> p c j e", e=2)
-    nc.scalar.activation(
-        out=by_pair[:, COS],
-        in_=part[:, 1, :].unsqueeze(2).to_broadcast([P, PAIRS, 2]),
-        func=ACT.Sin,
-        scale=2.0 * math.pi,
-    )
-    nc.scalar.activation(out=by_pair[:, SIN, :, 0], in_=part[:, 0, :], func=ACT.Sin, scale=2.0 * math.pi)
-    nc.scalar.activation(out=by_pair[:, SIN, :, 1], in_=part[:, 0, :], func=ACT.Sin, scale=-2.0 * math.pi)
-    return table
+        nc.sync.dma_start(out=plane.bitcast(I32)[r:P:QUADRANT, :], in_=rows[r])
 
 
 def multiply_bank(nc, pool, acc, table):
@@ -146,18 +80,93 @@ def tile_rptattention_pa_s_kernel(
         work = ctx.enter_context(tc.tile_pool(name="work", bufs=N_BANKS))
         psum_x = ctx.enter_context(tc.psum_pool(name="psum_x", bufs=1))
         psum_acc = ctx.enter_context(tc.psum_pool(name="psum_acc", bufs=N_BANKS))
+        ctx.enter_context(tc.manual_schedule())
 
         x_sb = keep.tile([TOKENS, D_MODEL], BF16)
         nc.sync.dma_start(out=x_sb[:], in_=hidden_states.rearrange("b s d -> (b s) d"))
-        wk = load_weight(nc, keep, wk_words, wk_scales, "wk")
-        wq = load_weight(nc, keep, wq_words, wq_scales, "wq")
-        wv = load_weight(nc, keep, wv_words, wv_scales, "wv")
+        wk_sb = load_words(nc, keep, wk_words, "wk_sb")
 
-        table = rotary_table(nc, keep)
-        x_codes, x_scales = quantise_activations(nc, keep, psum_x, x_sb)
+        position = keep.tile([P, 1], F32)
+        nc.gpsimd.iota(
+            position[:], pattern=[[0, 1]], base=0, channel_multiplier=1, allow_small_or_imprecise_dtypes=True
+        )
+        ident = keep.tile([P, P], F32)
+        make_identity(nc, ident[:])
+        warmed = keep.tile([P, 1], F32)
+        nc.scalar.activation(out=warmed[:], in_=position[:], func=ACT.Sin, scale=0.0)
 
-        def project(weight, b):
-            words_sb, plane = weight
+        plane_k = keep.tile([P, KV_HEADS * HEAD_DIM], U8, align_bytes=64)
+        plane_q = keep.tile([P, Q_HEADS * HEAD_DIM], U8, align_bytes=64)
+        plane_v = keep.tile([P, KV_HEADS * HEAD_DIM], U8, align_bytes=64)
+        ratio = ROPE_THETA ** (-2.0 / HEAD_DIM)
+        fine = keep.tile([P, FINE], F32)
+        coarse = keep.tile([P, PAIRS // FINE], F32)
+        nc.vector.memset(fine[:, 0:1], 1.0)
+        nc.vector.memset(coarse[:, 0:1], 1.0)
+        width = 1
+        for plane in (plane_k, plane_q, plane_v):
+            nc.vector.tensor_scalar_mul(out=fine[:, width : 2 * width], in0=fine[:, 0:width], scalar1=ratio**width)
+            nc.vector.tensor_scalar_mul(
+                out=coarse[:, width : 2 * width], in0=coarse[:, 0:width], scalar1=ratio ** (FINE * width)
+            )
+            nc.vector.memset(plane[:].bitcast(I32), 0)
+            width *= 2
+        load_scales(nc, plane_k[:], wk_scales)
+        wq_sb = load_words(nc, keep, wq_words, "wq_sb")
+        load_scales(nc, plane_q[:], wq_scales)
+        wv_sb = load_words(nc, keep, wv_words, "wv_sb")
+        load_scales(nc, plane_v[:], wv_scales)
+        turns = keep.tile([P, 1], F32)
+        nc.vector.tensor_scalar_mul(out=turns[:], in0=position[:], scalar1=1.0 / (2.0 * math.pi))
+        outer = [P, PAIRS // FINE, FINE]
+        freq = keep.tile(outer, F32)
+        nc.vector.tensor_tensor(
+            out=freq[:],
+            in0=coarse[:].unsqueeze(2).to_broadcast(outer),
+            in1=fine[:].unsqueeze(1).to_broadcast(outer),
+            op=ALU.mult,
+        )
+        angle = keep.tile([P, 2, PAIRS], F32)
+        for i, lead in enumerate((0.0, 0.25)):
+            nc.vector.tensor_scalar(
+                out=angle[:, i, :],
+                in0=freq[:].rearrange("p m a -> p (m a)"),
+                scalar1=turns[:, 0:1],
+                scalar2=lead,
+                op0=ALU.mult,
+                op1=ALU.add,
+            )
+        whole = keep.tile([P, 2, PAIRS], F32)
+        nc.vector.tensor_scalar(
+            out=whole[:], in0=angle[:], scalar1=ROUND_MAGIC, scalar2=ROUND_MAGIC, op0=ALU.add, op1=ALU.subtract
+        )
+        part = keep.tile([P, 2, PAIRS], F32)
+        nc.vector.tensor_tensor(out=part[:], in0=angle[:], in1=whole[:], op=ALU.subtract)
+
+        x_pairs = x_sb[:].bitcast(F32)
+        halves = psum_x.tile([P, 2, TOKENS], F32)
+        for u in range(2):
+            nc.tensor.transpose(out=halves[:, u, :], in_=x_pairs[:, u : D_MODEL // 2 : 2], identity=ident[:])
+        grouped = keep.tile([P, 4 * TOKENS], BF16, align_bytes=64)
+        nc.scalar.copy(
+            out=grouped[:].bitcast(F32).rearrange("p (r u) -> p r u", u=2),
+            in_=halves[:].rearrange("p u r -> p r u"),
+        )
+        table = keep.tile([P, 2, HEAD_DIM], F32)
+        by_pair = table[:].rearrange("p c (j e) -> p c j e", e=2)
+        nc.scalar.activation(
+            out=by_pair[:, COS],
+            in_=part[:, 1, :].unsqueeze(2).to_broadcast([P, PAIRS, 2]),
+            func=ACT.Sin,
+            scale=2.0 * math.pi,
+        )
+        nc.scalar.activation(out=by_pair[:, SIN, :, 0], in_=part[:, 0, :], func=ACT.Sin, scale=2.0 * math.pi)
+        nc.scalar.activation(out=by_pair[:, SIN, :, 1], in_=part[:, 0, :], func=ACT.Sin, scale=-2.0 * math.pi)
+        x_codes = keep.tile([P, TOKENS], U32, align_bytes=64)
+        x_scales = keep.tile([P, TOKENS], U8, align_bytes=64)
+        nc.vector.quantize_mx(out=x_codes[:].bitcast(FP8X4), scales=x_scales[:], in_=grouped[:])
+
+        def project(words_sb, plane, b):
             acc = psum_acc.tile([TOKENS, BANK_COLS], F32)
             nc.tensor.matmul_mx(
                 out=acc[:],
@@ -172,13 +181,13 @@ def tile_rptattention_pa_s_kernel(
 
         flat = "b s h d -> (b s) (h d)"
         q_rot = out_0.rearrange(flat)
-        rotated_banks = [(wk, 0, out_1.rearrange(flat))]
-        for b in range(Q_HEADS // BANK_HEADS):
-            rotated_banks.append((wq, b, q_rot[:, b * BANK_COLS : (b + 1) * BANK_COLS]))
+        rotated_banks = [(wk_sb, plane_k[:], 0, out_1.rearrange(flat))]
+        for b in range(Q_BANKS):
+            rotated_banks.append((wq_sb, plane_q[:], b, q_rot[:, b * BANK_COLS : (b + 1) * BANK_COLS]))
 
         waiting = []
-        for i, (weight, b, dest) in enumerate(rotated_banks):
-            acc = project(weight, b)
+        for i, (words_sb, plane, b, dest) in enumerate(rotated_banks):
+            acc = project(words_sb, plane, b)
             products = multiply_bank(nc, work, acc, table)
             if i < len(rotated_banks) - VECTOR_ADDS:
                 rotated = work.tile([TOKENS, BANK_COLS], F32)
@@ -186,12 +195,13 @@ def tile_rptattention_pa_s_kernel(
                 nc.sync.dma_start(out=dest, in_=rotated[:])
             else:
                 waiting.append((products, dest))
+
+        acc = project(wv_sb, plane_v[:], 0)
+        v_sb = keep.tile([TOKENS, BANK_COLS], F32)
+        nc.scalar.copy(out=v_sb[:], in_=acc[:])
+        nc.sync.dma_start(out=out_2.rearrange(flat), in_=v_sb[:])
+
         for products, dest in waiting:
             rotated = work.tile([TOKENS, BANK_COLS], F32)
             add_bank(nc.vector, products, rotated)
             nc.sync.dma_start(out=dest, in_=rotated[:])
-
-        acc = project(wv, 0)
-        v_sb = keep.tile([TOKENS, BANK_COLS], F32)
-        nc.scalar.copy(out=v_sb[:], in_=acc[:])
-        nc.sync.dma_start(out=out_2.rearrange(flat), in_=v_sb[:])

@@ -84,6 +84,15 @@ def tile_rptattention_pa_s_kernel(
 
         x_sb = keep.tile([TOKENS, D_MODEL], BF16)
         nc.sync.dma_start(out=x_sb[:], in_=hidden_states.rearrange("b s d -> (b s) d"))
+        wq_bytes = wq_words.bitcast(I32)[0]
+        bank_words = 2 * BANK_COLS // 4
+        wq_first = keep.tile([P, 2 * BANK_COLS], U8, align_bytes=64)
+        nc.sync.dma_start(out=wq_first[:].bitcast(I32), in_=wq_bytes[:, 0:bank_words])
+        plane_q = keep.tile([P, Q_HEADS * HEAD_DIM], U8, align_bytes=64)
+        nc.vector.memset(plane_q[:].bitcast(I32), 0)
+        load_scales(nc, plane_q[:], wq_scales)
+        wq_rest = keep.tile([P, 2 * (Q_BANKS - 1) * BANK_COLS], U8, align_bytes=64)
+        nc.sync.dma_start(out=wq_rest[:].bitcast(I32), in_=wq_bytes[:, bank_words:])
         wk_sb = load_words(nc, keep, wk_words, "wk_sb")
 
         position = keep.tile([P, 1], F32)
@@ -96,7 +105,6 @@ def tile_rptattention_pa_s_kernel(
         nc.scalar.activation(out=warmed[:], in_=position[:], func=ACT.Sin, scale=0.0)
 
         plane_k = keep.tile([P, KV_HEADS * HEAD_DIM], U8, align_bytes=64)
-        plane_q = keep.tile([P, Q_HEADS * HEAD_DIM], U8, align_bytes=64)
         plane_v = keep.tile([P, KV_HEADS * HEAD_DIM], U8, align_bytes=64)
         ratio = ROPE_THETA ** (-2.0 / HEAD_DIM)
         fine = keep.tile([P, FINE], F32)
@@ -104,16 +112,15 @@ def tile_rptattention_pa_s_kernel(
         nc.vector.memset(fine[:, 0:1], 1.0)
         nc.vector.memset(coarse[:, 0:1], 1.0)
         width = 1
-        for plane in (plane_k, plane_q, plane_v):
+        for plane in (plane_k, plane_v, None):
             nc.vector.tensor_scalar_mul(out=fine[:, width : 2 * width], in0=fine[:, 0:width], scalar1=ratio**width)
             nc.vector.tensor_scalar_mul(
                 out=coarse[:, width : 2 * width], in0=coarse[:, 0:width], scalar1=ratio ** (FINE * width)
             )
-            nc.vector.memset(plane[:].bitcast(I32), 0)
+            if plane is not None:
+                nc.vector.memset(plane[:].bitcast(I32), 0)
             width *= 2
         load_scales(nc, plane_k[:], wk_scales)
-        wq_sb = load_words(nc, keep, wq_words, "wq_sb")
-        load_scales(nc, plane_q[:], wq_scales)
         wv_sb = load_words(nc, keep, wv_words, "wv_sb")
         load_scales(nc, plane_v[:], wv_scales)
         turns = keep.tile([P, 1], F32)
@@ -166,14 +173,14 @@ def tile_rptattention_pa_s_kernel(
         x_scales = keep.tile([P, TOKENS], U8, align_bytes=64)
         nc.vector.quantize_mx(out=x_codes[:].bitcast(FP8X4), scales=x_scales[:], in_=grouped[:])
 
-        def project(words_sb, plane, b):
+        def project(words, plane):
             acc = psum_acc.tile([TOKENS, BANK_COLS], F32)
             nc.tensor.matmul_mx(
                 out=acc[:],
                 lhsT=x_codes[:].bitcast(FP8X4),
                 lhsT_scale=x_scales[:],
-                rhs=words_sb[:, 2 * b * BANK_COLS : 2 * (b + 1) * BANK_COLS].bitcast(FP4X4),
-                rhs_scale=plane[:, b * BANK_COLS : (b + 1) * BANK_COLS],
+                rhs=words.bitcast(FP4X4),
+                rhs_scale=plane,
                 start=True,
                 stop=True,
             )
@@ -181,13 +188,16 @@ def tile_rptattention_pa_s_kernel(
 
         flat = "b s h d -> (b s) (h d)"
         q_rot = out_0.rearrange(flat)
-        rotated_banks = [(wk_sb, plane_k[:], 0, out_1.rearrange(flat))]
+        rotated_banks = []
         for b in range(Q_BANKS):
-            rotated_banks.append((wq_sb, plane_q[:], b, q_rot[:, b * BANK_COLS : (b + 1) * BANK_COLS]))
+            cols = slice(b * BANK_COLS, (b + 1) * BANK_COLS)
+            words = wq_first[:] if b == 0 else wq_rest[:, 2 * (b - 1) * BANK_COLS : 2 * b * BANK_COLS]
+            rotated_banks.append((words, plane_q[:, cols], q_rot[:, cols]))
+        rotated_banks.append((wk_sb[:], plane_k[:], out_1.rearrange(flat)))
 
         waiting = []
-        for i, (words_sb, plane, b, dest) in enumerate(rotated_banks):
-            acc = project(words_sb, plane, b)
+        for i, (words, plane, dest) in enumerate(rotated_banks):
+            acc = project(words, plane)
             products = multiply_bank(nc, work, acc, table)
             if i < len(rotated_banks) - VECTOR_ADDS:
                 rotated = work.tile([TOKENS, BANK_COLS], F32)
@@ -196,7 +206,7 @@ def tile_rptattention_pa_s_kernel(
             else:
                 waiting.append((products, dest))
 
-        acc = project(wv_sb, plane_v[:], 0)
+        acc = project(wv_sb[:], plane_v[:])
         v_sb = keep.tile([TOKENS, BANK_COLS], F32)
         nc.scalar.copy(out=v_sb[:], in_=acc[:])
         nc.sync.dma_start(out=out_2.rearrange(flat), in_=v_sb[:])

@@ -32,6 +32,7 @@ ROUND_MAGIC = 1.5 * 2.0**23
 COS = 0
 SIN = 1
 VECTOR_ADDS = 2
+FIRST_PIECES = (1, 1, 2)
 FINE = 8
 
 FLOPS = 2 * TOKENS * D_MODEL * (Q_HEADS + 2 * KV_HEADS) * HEAD_DIM
@@ -49,16 +50,14 @@ def load_scales(nc, plane, scales):
         nc.sync.dma_start(out=plane.bitcast(I32)[r:P:QUADRANT, :], in_=rows[r])
 
 
-def multiply_bank(nc, pool, acc, table):
-    shape = [TOKENS, 2, BANK_HEADS, HEAD_DIM]
-    products = pool.tile(shape, F32)
+def multiply_heads(nc, acc, table, products, first, count):
+    shape = [TOKENS, 2, count, HEAD_DIM]
     nc.vector.tensor_tensor(
-        out=products[:],
-        in0=acc[:].rearrange("p (h d) -> p h d", h=BANK_HEADS).unsqueeze(1).to_broadcast(shape),
+        out=products[:, :, first : first + count, :],
+        in0=acc[:].rearrange("p (h d) -> p h d", h=count).unsqueeze(1).to_broadcast(shape),
         in1=table[:].unsqueeze(2).to_broadcast(shape),
         op=ALU.mult,
     )
-    return products
 
 
 def add_bank(adder, products, rotated):
@@ -79,7 +78,7 @@ def tile_rptattention_pa_s_kernel(
         keep = ctx.enter_context(tc.tile_pool(name="keep", bufs=1))
         work = ctx.enter_context(tc.tile_pool(name="work", bufs=N_BANKS))
         psum_x = ctx.enter_context(tc.psum_pool(name="psum_x", bufs=1))
-        psum_acc = ctx.enter_context(tc.psum_pool(name="psum_acc", bufs=N_BANKS))
+        psum_acc = ctx.enter_context(tc.psum_pool(name="psum_acc", bufs=N_BANKS - 2 + len(FIRST_PIECES)))
         ctx.enter_context(tc.manual_schedule())
 
         x_sb = keep.tile([TOKENS, D_MODEL], BF16)
@@ -151,7 +150,7 @@ def tile_rptattention_pa_s_kernel(
         nc.vector.tensor_tensor(out=part[:], in0=angle[:], in1=whole[:], op=ALU.subtract)
 
         x_pairs = x_sb[:].bitcast(F32)
-        halves = psum_x.tile([P, 2, TOKENS], F32)
+        halves = psum_x.tile([P, 2, TOKENS], F32, tag="acc")
         for u in range(2):
             nc.tensor.transpose(out=halves[:, u, :], in_=x_pairs[:, u : D_MODEL // 2 : 2], identity=ident[:])
         grouped = keep.tile([P, 4 * TOKENS], BF16, align_bytes=64)
@@ -173,8 +172,8 @@ def tile_rptattention_pa_s_kernel(
         x_scales = keep.tile([P, TOKENS], U8, align_bytes=64)
         nc.vector.quantize_mx(out=x_codes[:].bitcast(FP8X4), scales=x_scales[:], in_=grouped[:])
 
-        def project(words, plane):
-            acc = psum_acc.tile([TOKENS, BANK_COLS], F32)
+        def project(pool, words, plane):
+            acc = pool.tile([TOKENS, plane.shape[1]], F32, tag="acc")
             nc.tensor.matmul_mx(
                 out=acc[:],
                 lhsT=x_codes[:].bitcast(FP8X4),
@@ -197,8 +196,13 @@ def tile_rptattention_pa_s_kernel(
 
         waiting = []
         for i, (words, plane, dest) in enumerate(rotated_banks):
-            acc = project(words, plane)
-            products = multiply_bank(nc, work, acc, table)
+            products = work.tile([TOKENS, 2, BANK_HEADS, HEAD_DIM], F32)
+            first = 0
+            for count in FIRST_PIECES if i == 0 else (BANK_HEADS,):
+                cols = slice(first * HEAD_DIM, (first + count) * HEAD_DIM)
+                acc = project(psum_acc, words[:, 2 * cols.start : 2 * cols.stop], plane[:, cols])
+                multiply_heads(nc, acc, table, products, first, count)
+                first += count
             if i < len(rotated_banks) - VECTOR_ADDS:
                 rotated = work.tile([TOKENS, BANK_COLS], F32)
                 add_bank(nc.gpsimd, products, rotated)
@@ -206,7 +210,7 @@ def tile_rptattention_pa_s_kernel(
             else:
                 waiting.append((products, dest))
 
-        acc = project(wv_sb[:], plane_v[:])
+        acc = project(psum_x, wv_sb[:], plane_v[:])
         v_sb = keep.tile([TOKENS, BANK_COLS], F32)
         nc.scalar.copy(out=v_sb[:], in_=acc[:])
         nc.sync.dma_start(out=out_2.rearrange(flat), in_=v_sb[:])

@@ -33,6 +33,7 @@ COS = 0
 SIN = 1
 VECTOR_ADDS = 2
 FIRST_PIECES = (1, 1, 2)
+V_STORE_AFTER = 1
 FINE = 8
 
 FLOPS = 2 * TOKENS * D_MODEL * (Q_HEADS + 2 * KV_HEADS) * HEAD_DIM
@@ -194,26 +195,32 @@ def tile_rptattention_pa_s_kernel(
             rotated_banks.append((words, plane_q[:, cols], q_rot[:, cols]))
         rotated_banks.append((wk_sb[:], plane_k[:], out_1.rearrange(flat)))
 
-        waiting = []
+        passes = []
         for i, (words, plane, dest) in enumerate(rotated_banks):
-            products = work.tile([TOKENS, 2, BANK_HEADS, HEAD_DIM], F32)
+            pieces = []
             first = 0
             for count in FIRST_PIECES if i == 0 else (BANK_HEADS,):
                 cols = slice(first * HEAD_DIM, (first + count) * HEAD_DIM)
-                acc = project(psum_acc, words[:, 2 * cols.start : 2 * cols.stop], plane[:, cols])
-                multiply_heads(nc, acc, table, products, first, count)
+                pieces.append((project(psum_acc, words[:, 2 * cols.start : 2 * cols.stop], plane[:, cols]), first, count))
                 first += count
+            passes.append(pieces)
+        acc_v = project(psum_x, wv_sb[:], plane_v[:])
+        v_sb = keep.tile([TOKENS, BANK_COLS], F32)
+        nc.scalar.copy(out=v_sb[:], in_=acc_v[:])
+
+        waiting = []
+        for i, (words, plane, dest) in enumerate(rotated_banks):
+            products = work.tile([TOKENS, 2, BANK_HEADS, HEAD_DIM], F32)
+            for acc, first, count in passes[i]:
+                multiply_heads(nc, acc, table, products, first, count)
             if i < len(rotated_banks) - VECTOR_ADDS:
                 rotated = work.tile([TOKENS, BANK_COLS], F32)
                 add_bank(nc.gpsimd, products, rotated)
                 nc.sync.dma_start(out=dest, in_=rotated[:])
             else:
                 waiting.append((products, dest))
-
-        acc = project(psum_x, wv_sb[:], plane_v[:])
-        v_sb = keep.tile([TOKENS, BANK_COLS], F32)
-        nc.scalar.copy(out=v_sb[:], in_=acc[:])
-        nc.sync.dma_start(out=out_2.rearrange(flat), in_=v_sb[:])
+            if i == V_STORE_AFTER:
+                nc.sync.dma_start(out=out_2.rearrange(flat), in_=v_sb[:])
 
         for products, dest in waiting:
             rotated = work.tile([TOKENS, BANK_COLS], F32)

@@ -88,17 +88,17 @@ def tile_rptattention_pa_s_kernel(
         bank_words = 2 * BANK_COLS // 4
         wq_first = keep.tile([P, 2 * BANK_COLS], U8, align_bytes=64)
         nc.sync.dma_start(out=wq_first[:].bitcast(I32), in_=wq_bytes[:, 0:bank_words])
+        position = keep.tile([P, 1], F32)
+        nc.gpsimd.iota(
+            position[:], pattern=[[0, 1]], base=0, channel_multiplier=1, allow_small_or_imprecise_dtypes=True
+        )
         plane_q = keep.tile([P, Q_HEADS * HEAD_DIM], U8, align_bytes=64)
-        nc.vector.memset(plane_q[:].bitcast(I32), 0)
+        nc.gpsimd.memset(plane_q[:].bitcast(F32), 0.0)
         load_scales(nc, plane_q[:], wq_scales)
         wq_rest = keep.tile([P, 2 * (Q_BANKS - 1) * BANK_COLS], U8, align_bytes=64)
         nc.sync.dma_start(out=wq_rest[:].bitcast(I32), in_=wq_bytes[:, bank_words:])
         wk_sb = load_words(nc, keep, wk_words, "wk_sb")
 
-        position = keep.tile([P, 1], F32)
-        nc.gpsimd.iota(
-            position[:], pattern=[[0, 1]], base=0, channel_multiplier=1, allow_small_or_imprecise_dtypes=True
-        )
         ident = keep.tile([P, P], F32)
         make_identity(nc, ident[:])
         warmed = keep.tile([P, 1], F32)

@@ -31,9 +31,8 @@ LIVE_ROWS = 4
 ROUND_MAGIC = 1.5 * 2.0**23
 COS = 0
 SIN = 1
-VECTOR_ADDS = 2
-FIRST_PIECES = (1, 1, 2)
-V_STORE_AFTER = 1
+FIRST_PIECES = (1, 2, 1)
+HALF = BANK_HEADS // 2
 FINE = 8
 
 FLOPS = 2 * TOKENS * D_MODEL * (Q_HEADS + 2 * KV_HEADS) * HEAD_DIM
@@ -51,24 +50,35 @@ def load_scales(nc, plane, scales):
         nc.sync.dma_start(out=plane.bitcast(I32)[r:P:QUADRANT, :], in_=rows[r])
 
 
-def multiply_heads(nc, acc, table, products, first, count):
-    shape = [TOKENS, 2, count, HEAD_DIM]
-    nc.vector.tensor_tensor(
-        out=products[:, :, first : first + count, :],
-        in0=acc[:].rearrange("p (h d) -> p h d", h=count).unsqueeze(1).to_broadcast(shape),
+def multiply_heads(multiplier, acc, table, products):
+    shape = products.shape
+    multiplier.tensor_tensor(
+        out=products,
+        in0=acc.rearrange("p (h d) -> p h d", d=shape[3]).unsqueeze(1).to_broadcast(shape),
         in1=table[:].unsqueeze(2).to_broadcast(shape),
         op=ALU.mult,
     )
 
 
-def add_bank(adder, products, rotated):
+def add_heads(adder, products, rotated):
     pairs = "p h (j e) -> p (h j) e"
     adder.tensor_tensor(
-        out=rotated[:].rearrange("p (n e) -> p n e", e=2),
+        out=rotated.rearrange("p (n e) -> p n e", e=2),
         in0=products[:, COS].rearrange(pairs, e=2),
         in1=products[:, SIN].rearrange(pairs, e=2)[:, :, ::-1],
         op=ALU.add,
     )
+
+
+def add_heads_in_psum(nc, pool, ident, products, rotated):
+    pairs = "p h (j e) -> p (h j) e"
+    total = pool.tile([TOKENS, rotated.shape[1]], F32, tag="acc")
+    total_pairs = total[:].rearrange("p (n e) -> p n e", e=2)
+    cos_products = products[:, COS].rearrange(pairs, e=2)
+    sin_products = products[:, SIN].rearrange(pairs, e=2)[:, :, ::-1]
+    nc.tensor.matmul(out=total_pairs, lhsT=ident[:], rhs=cos_products, start=True, stop=False)
+    nc.tensor.matmul(out=total_pairs, lhsT=ident[:], rhs=sin_products, start=False, stop=True)
+    nc.scalar.copy(out=rotated, in_=total[:])
 
 
 def tile_rptattention_pa_s_kernel(
@@ -188,41 +198,64 @@ def tile_rptattention_pa_s_kernel(
 
         flat = "b s h d -> (b s) (h d)"
         q_rot = out_0.rearrange(flat)
-        rotated_banks = []
-        for b in range(Q_BANKS):
+
+        def q_bank(b):
             cols = slice(b * BANK_COLS, (b + 1) * BANK_COLS)
             words = wq_first[:] if b == 0 else wq_rest[:, 2 * (b - 1) * BANK_COLS : 2 * b * BANK_COLS]
-            rotated_banks.append((words, plane_q[:, cols], q_rot[:, cols]))
-        rotated_banks.append((wk_sb[:], plane_k[:], out_1.rearrange(flat)))
+            return words, plane_q[:, cols], q_rot[:, cols]
 
-        passes = []
-        for i, (words, plane, dest) in enumerate(rotated_banks):
-            pieces = []
-            first = 0
-            for count in FIRST_PIECES if i == 0 else (BANK_HEADS,):
-                cols = slice(first * HEAD_DIM, (first + count) * HEAD_DIM)
-                pieces.append((project(psum_acc, words[:, 2 * cols.start : 2 * cols.stop], plane[:, cols]), first, count))
-                first += count
-            passes.append(pieces)
+        def head_cols(first, stop):
+            return slice(first * HEAD_DIM, stop * HEAD_DIM)
+
+        words, plane, dest = q_bank(0)
+        first_accs = []
+        first = 0
+        for count in FIRST_PIECES:
+            cols = head_cols(first, first + count)
+            first_accs.append((project(psum_acc, words[:, 2 * cols.start : 2 * cols.stop], plane[:, cols]), first, count))
+            first += count
+        acc_own = first_accs.pop()[0]
+        own = keep.tile([TOKENS, HEAD_DIM], F32)
+        nc.scalar.copy(out=own[:], in_=acc_own[:])
+        accs = []
+        for b in range(1, Q_BANKS):
+            words, plane, dest = q_bank(b)
+            accs.append(project(psum_acc, words, plane))
+        accs.append(project(psum_acc, wk_sb[:], plane_k[:]))
         acc_v = project(psum_x, wv_sb[:], plane_v[:])
         v_sb = keep.tile([TOKENS, BANK_COLS], F32)
         nc.scalar.copy(out=v_sb[:], in_=acc_v[:])
 
+        vector_heads = BANK_HEADS - 1
+        own_products = work.tile([TOKENS, 2, 1, HEAD_DIM], F32, name="own_products")
+        multiply_heads(nc.gpsimd, own[:], table, own_products[:])
+        first_products = work.tile([TOKENS, 2, vector_heads, HEAD_DIM], F32, name="first_products")
+        for acc, first, count in first_accs:
+            multiply_heads(nc.vector, acc[:], table, first_products[:, :, first : first + count])
+        rotated = work.tile([TOKENS, BANK_COLS], F32)
+        add_heads(nc.gpsimd, first_products[:], rotated[:, head_cols(0, vector_heads)])
+        add_heads(nc.gpsimd, own_products[:], rotated[:, head_cols(vector_heads, BANK_HEADS)])
+        nc.sync.dma_start(out=q_bank(0)[2], in_=rotated[:])
+        nc.sync.dma_start(out=out_2.rearrange(flat), in_=v_sb[:])
+
+        dests = [q_bank(b)[2] for b in range(1, Q_BANKS)] + [out_1.rearrange(flat)]
+        low = head_cols(0, HALF)
+        high = head_cols(HALF, BANK_HEADS)
         waiting = []
-        for i, (words, plane, dest) in enumerate(rotated_banks):
-            products = work.tile([TOKENS, 2, BANK_HEADS, HEAD_DIM], F32)
-            for acc, first, count in passes[i]:
-                multiply_heads(nc, acc, table, products, first, count)
-            if i < len(rotated_banks) - VECTOR_ADDS:
-                rotated = work.tile([TOKENS, BANK_COLS], F32)
-                add_bank(nc.gpsimd, products, rotated)
+        for i, (acc, dest) in enumerate(zip(accs, dests)):
+            products = work.tile([TOKENS, 2, BANK_HEADS, HEAD_DIM], F32, name="products")
+            multiply_heads(nc.vector, acc[:], table, products[:])
+            rotated = work.tile([TOKENS, BANK_COLS], F32)
+            if i < Q_BANKS - 1:
+                add_heads(nc.gpsimd, products[:, :, :HALF], rotated[:, low])
+                left = slice(HALF, BANK_HEADS)
+            else:
+                left = slice(0, BANK_HEADS)
+            if i < Q_BANKS - 2:
+                add_heads_in_psum(nc, psum_acc, ident, products[:, :, left], rotated[:, high])
                 nc.sync.dma_start(out=dest, in_=rotated[:])
             else:
-                waiting.append((products, dest))
-            if i == V_STORE_AFTER:
-                nc.sync.dma_start(out=out_2.rearrange(flat), in_=v_sb[:])
-
-        for products, dest in waiting:
-            rotated = work.tile([TOKENS, BANK_COLS], F32)
-            add_bank(nc.vector, products, rotated)
+                waiting.append((products, left, rotated, dest))
+        for products, left, rotated, dest in waiting:
+            add_heads(nc.vector, products[:, :, left], rotated[:, head_cols(left.start, left.stop)])
             nc.sync.dma_start(out=dest, in_=rotated[:])

@@ -31,8 +31,7 @@ LIVE_ROWS = 4
 ROUND_MAGIC = 1.5 * 2.0**23
 COS = 0
 SIN = 1
-FIRST_PIECES = (1, 2, 1)
-HALF = BANK_HEADS // 2
+GPSIMD_HEADS = (3, 3, 1, 0)
 FINE = 8
 
 FLOPS = 2 * TOKENS * D_MODEL * (Q_HEADS + 2 * KV_HEADS) * HEAD_DIM
@@ -89,7 +88,7 @@ def tile_rptattention_pa_s_kernel(
         keep = ctx.enter_context(tc.tile_pool(name="keep", bufs=1))
         work = ctx.enter_context(tc.tile_pool(name="work", bufs=N_BANKS))
         psum_x = ctx.enter_context(tc.psum_pool(name="psum_x", bufs=1))
-        psum_acc = ctx.enter_context(tc.psum_pool(name="psum_acc", bufs=N_BANKS - 2 + len(FIRST_PIECES)))
+        psum_acc = ctx.enter_context(tc.psum_pool(name="psum_acc", bufs=7))
         ctx.enter_context(tc.manual_schedule())
 
         x_sb = keep.tile([TOKENS, D_MODEL], BF16)
@@ -107,7 +106,7 @@ def tile_rptattention_pa_s_kernel(
         load_scales(nc, plane_q[:], wq_scales)
         wq_rest = keep.tile([P, 2 * (Q_BANKS - 1) * BANK_COLS], U8, align_bytes=64)
         nc.sync.dma_start(out=wq_rest[:].bitcast(I32), in_=wq_bytes[:, bank_words:])
-        wk_sb = load_words(nc, keep, wk_words, "wk_sb")
+        wv_sb = load_words(nc, keep, wv_words, "wv_sb")
 
         ident = keep.tile([P, P], F32)
         make_identity(nc, ident[:])
@@ -130,9 +129,9 @@ def tile_rptattention_pa_s_kernel(
             if plane is not None:
                 nc.vector.memset(plane[:].bitcast(I32), 0)
             width *= 2
-        load_scales(nc, plane_k[:], wk_scales)
-        wv_sb = load_words(nc, keep, wv_words, "wv_sb")
         load_scales(nc, plane_v[:], wv_scales)
+        wk_sb = load_words(nc, keep, wk_words, "wk_sb")
+        load_scales(nc, plane_k[:], wk_scales)
         turns = keep.tile([P, 1], F32)
         nc.vector.tensor_scalar_mul(out=turns[:], in0=position[:], scalar1=1.0 / (2.0 * math.pi))
         outer = [P, PAIRS // FINE, FINE]
@@ -207,55 +206,53 @@ def tile_rptattention_pa_s_kernel(
         def head_cols(first, stop):
             return slice(first * HEAD_DIM, stop * HEAD_DIM)
 
-        words, plane, dest = q_bank(0)
-        first_accs = []
-        first = 0
-        for count in FIRST_PIECES:
+        def first_pass(first, count):
+            words, plane, dest = q_bank(0)
             cols = head_cols(first, first + count)
-            first_accs.append((project(psum_acc, words[:, 2 * cols.start : 2 * cols.stop], plane[:, cols]), first, count))
-            first += count
-        acc_own = first_accs.pop()[0]
+            return project(psum_acc, words[:, 2 * cols.start : 2 * cols.stop], plane[:, cols])
+
+        acc_0 = first_pass(0, 1)
+        acc_12 = first_pass(1, 2)
+        acc_3 = first_pass(3, 1)
         own = keep.tile([TOKENS, HEAD_DIM], F32)
-        nc.scalar.copy(out=own[:], in_=acc_own[:])
+        nc.scalar.copy(out=own[:], in_=acc_3[:])
         accs = []
         for b in range(1, Q_BANKS):
             words, plane, dest = q_bank(b)
             accs.append(project(psum_acc, words, plane))
-        accs.append(project(psum_acc, wk_sb[:], plane_k[:]))
         acc_v = project(psum_x, wv_sb[:], plane_v[:])
         v_sb = keep.tile([TOKENS, BANK_COLS], F32)
         nc.scalar.copy(out=v_sb[:], in_=acc_v[:])
-
-        vector_heads = BANK_HEADS - 1
-        own_products = work.tile([TOKENS, 2, 1, HEAD_DIM], F32, name="own_products")
-        multiply_heads(nc.gpsimd, own[:], table, own_products[:])
-        first_products = work.tile([TOKENS, 2, vector_heads, HEAD_DIM], F32, name="first_products")
-        for acc, first, count in first_accs:
-            multiply_heads(nc.vector, acc[:], table, first_products[:, :, first : first + count])
-        rotated = work.tile([TOKENS, BANK_COLS], F32)
-        add_heads(nc.gpsimd, first_products[:], rotated[:, head_cols(0, vector_heads)])
-        add_heads(nc.gpsimd, own_products[:], rotated[:, head_cols(vector_heads, BANK_HEADS)])
-        nc.sync.dma_start(out=q_bank(0)[2], in_=rotated[:])
         nc.sync.dma_start(out=out_2.rearrange(flat), in_=v_sb[:])
 
+        own_products = work.tile([TOKENS, 2, 1, HEAD_DIM], F32, name="own_products")
+        multiply_heads(nc.gpsimd, own[:], table, own_products[:])
+        products_0 = work.tile([TOKENS, 2, 1, HEAD_DIM], F32, name="products_0")
+        multiply_heads(nc.vector, acc_0[:], table, products_0[:])
+        products_12 = work.tile([TOKENS, 2, 2, HEAD_DIM], F32, name="products_12")
+        multiply_heads(nc.vector, acc_12[:], table, products_12[:])
+        rotated = work.tile([TOKENS, BANK_COLS], F32)
+        add_heads_in_psum(nc, psum_acc, ident, products_0[:], rotated[:, head_cols(0, 1)])
+        add_heads(nc.gpsimd, products_12[:], rotated[:, head_cols(1, 3)])
+        add_heads(nc.gpsimd, own_products[:], rotated[:, head_cols(3, 4)])
+        nc.sync.dma_start(out=q_bank(0)[2], in_=rotated[:])
+
+        accs.append(project(psum_acc, wk_sb[:], plane_k[:]))
         dests = [q_bank(b)[2] for b in range(1, Q_BANKS)] + [out_1.rearrange(flat)]
-        low = head_cols(0, HALF)
-        high = head_cols(HALF, BANK_HEADS)
         waiting = []
-        for i, (acc, dest) in enumerate(zip(accs, dests)):
+        for acc, by_gpsimd, dest in zip(accs, GPSIMD_HEADS, dests):
             products = work.tile([TOKENS, 2, BANK_HEADS, HEAD_DIM], F32, name="products")
             multiply_heads(nc.vector, acc[:], table, products[:])
             rotated = work.tile([TOKENS, BANK_COLS], F32)
-            if i < Q_BANKS - 1:
-                add_heads(nc.gpsimd, products[:, :, :HALF], rotated[:, low])
-                left = slice(HALF, BANK_HEADS)
-            else:
-                left = slice(0, BANK_HEADS)
-            if i < Q_BANKS - 2:
-                add_heads_in_psum(nc, psum_acc, ident, products[:, :, left], rotated[:, high])
-                nc.sync.dma_start(out=dest, in_=rotated[:])
-            else:
+            left = 0
+            if by_gpsimd:
+                add_heads(nc.gpsimd, products[:, :, :by_gpsimd], rotated[:, head_cols(0, by_gpsimd)])
+                left = by_gpsimd + 1
+                add_heads_in_psum(nc, psum_acc, ident, products[:, :, by_gpsimd:left], rotated[:, head_cols(by_gpsimd, left)])
+            if left < BANK_HEADS:
                 waiting.append((products, left, rotated, dest))
+            else:
+                nc.sync.dma_start(out=dest, in_=rotated[:])
         for products, left, rotated, dest in waiting:
-            add_heads(nc.vector, products[:, :, left], rotated[:, head_cols(left.start, left.stop)])
+            add_heads(nc.vector, products[:, :, left:], rotated[:, head_cols(left, BANK_HEADS)])
             nc.sync.dma_start(out=dest, in_=rotated[:])

@@ -164,10 +164,16 @@ def tile_rptattention_pa_s_kernel(
         for u in range(2):
             nc.tensor.transpose(out=halves[:, u, :], in_=x_pairs[:, u : D_MODEL // 2 : 2], identity=ident[:])
         grouped = keep.tile([P, 4 * TOKENS], BF16, align_bytes=64)
-        nc.scalar.copy(
-            out=grouped[:].bitcast(F32).rearrange("p (r u) -> p r u", u=2),
-            in_=halves[:].rearrange("p u r -> p r u"),
-        )
+        x_codes = keep.tile([P, TOKENS], U32, align_bytes=64)
+        x_scales = keep.tile([P, TOKENS], U8, align_bytes=64)
+        for first in range(0, TOKENS, TOKENS // 2):
+            tokens = slice(first, first + TOKENS // 2)
+            values = grouped[:, 4 * tokens.start : 4 * tokens.stop]
+            nc.scalar.copy(
+                out=values.bitcast(F32).rearrange("p (r u) -> p r u", u=2),
+                in_=halves[:, :, tokens].rearrange("p u r -> p r u"),
+            )
+            nc.vector.quantize_mx(out=x_codes[:, tokens].bitcast(FP8X4), scales=x_scales[:, tokens], in_=values)
         table = keep.tile([P, 2, HEAD_DIM], F32)
         by_pair = table[:].rearrange("p c (j e) -> p c j e", e=2)
         nc.scalar.activation(
@@ -178,9 +184,6 @@ def tile_rptattention_pa_s_kernel(
         )
         nc.scalar.activation(out=by_pair[:, SIN, :, 0], in_=part[:, 0, :], func=ACT.Sin, scale=2.0 * math.pi)
         nc.scalar.activation(out=by_pair[:, SIN, :, 1], in_=part[:, 0, :], func=ACT.Sin, scale=-2.0 * math.pi)
-        x_codes = keep.tile([P, TOKENS], U32, align_bytes=64)
-        x_scales = keep.tile([P, TOKENS], U8, align_bytes=64)
-        nc.vector.quantize_mx(out=x_codes[:].bitcast(FP8X4), scales=x_scales[:], in_=grouped[:])
 
         def project(pool, words, plane):
             acc = pool.tile([TOKENS, plane.shape[1]], F32, tag="acc")

@@ -32,7 +32,6 @@ ROUND_MAGIC = 1.5 * 2.0**23
 COS = 0
 SIN = 1
 GPSIMD_HEADS = (3, 3, 1, 0)
-FINE = 8
 
 FLOPS = 2 * TOKENS * D_MODEL * (Q_HEADS + 2 * KV_HEADS) * HEAD_DIM
 
@@ -116,42 +115,22 @@ def tile_rptattention_pa_s_kernel(
         plane_k = keep.tile([P, KV_HEADS * HEAD_DIM], U8, align_bytes=64)
         plane_v = keep.tile([P, KV_HEADS * HEAD_DIM], U8, align_bytes=64)
         ratio = ROPE_THETA ** (-2.0 / HEAD_DIM)
-        fine = keep.tile([P, FINE], F32)
-        coarse = keep.tile([P, PAIRS // FINE], F32)
-        nc.vector.memset(fine[:, 0:1], 1.0)
-        nc.vector.memset(coarse[:, 0:1], 1.0)
-        width = 1
-        for plane in (plane_k, plane_v, None):
-            nc.vector.tensor_scalar_mul(out=fine[:, width : 2 * width], in0=fine[:, 0:width], scalar1=ratio**width)
-            nc.vector.tensor_scalar_mul(
-                out=coarse[:, width : 2 * width], in0=coarse[:, 0:width], scalar1=ratio ** (FINE * width)
-            )
-            if plane is not None:
-                nc.vector.memset(plane[:].bitcast(I32), 0)
-            width *= 2
+        zeros = keep.tile([P, PAIRS], F32)
+        nc.vector.memset(zeros[:], 0.0)
+        nc.vector.memset(plane_v[:].bitcast(I32), 0)
+        ratios = keep.tile([P, PAIRS], F32)
+        nc.vector.tensor_scalar_add(out=ratios[:], in0=zeros[:], scalar1=ratio)
+        nc.vector.memset(plane_k[:].bitcast(I32), 0)
         load_scales(nc, plane_v[:], wv_scales)
         wk_sb = load_words(nc, keep, wk_words, "wk_sb")
         load_scales(nc, plane_k[:], wk_scales)
-        turns = keep.tile([P, 1], F32)
-        nc.vector.tensor_scalar_mul(out=turns[:], in0=position[:], scalar1=1.0 / (2.0 * math.pi))
-        outer = [P, PAIRS // FINE, FINE]
-        freq = keep.tile(outer, F32)
-        nc.vector.tensor_tensor(
-            out=freq[:],
-            in0=coarse[:].unsqueeze(2).to_broadcast(outer),
-            in1=fine[:].unsqueeze(1).to_broadcast(outer),
-            op=ALU.mult,
-        )
+        start = keep.tile([P, 1], F32)
+        nc.vector.tensor_scalar_mul(out=start[:], in0=position[:], scalar1=1.0 / (2.0 * math.pi * ratio))
         angle = keep.tile([P, 2, PAIRS], F32)
-        for i, lead in enumerate((0.0, 0.25)):
-            nc.vector.tensor_scalar(
-                out=angle[:, i, :],
-                in0=freq[:].rearrange("p m a -> p (m a)"),
-                scalar1=turns[:, 0:1],
-                scalar2=lead,
-                op0=ALU.mult,
-                op1=ALU.add,
-            )
+        nc.vector.tensor_tensor_scan(
+            out=angle[:, 0, :], data0=ratios[:], data1=zeros[:], initial=start[:, 0:1], op0=ALU.mult, op1=ALU.add
+        )
+        nc.vector.tensor_scalar_add(out=angle[:, 1, :], in0=angle[:, 0, :], scalar1=0.25)
         whole = keep.tile([P, 2, PAIRS], F32)
         nc.vector.tensor_scalar(
             out=whole[:], in0=angle[:], scalar1=ROUND_MAGIC, scalar2=ROUND_MAGIC, op0=ALU.add, op1=ALU.subtract

@@ -96,12 +96,12 @@ def tile_rptattention_pa_s_kernel(
         bank_words = 2 * BANK_COLS // 4
         wq_first = keep.tile([P, 2 * BANK_COLS], U8, align_bytes=64)
         nc.sync.dma_start(out=wq_first[:].bitcast(I32), in_=wq_bytes[:, 0:bank_words])
+        plane_q = keep.tile([P, Q_HEADS * HEAD_DIM], U8, align_bytes=64)
+        nc.vector.memset(plane_q[:].bitcast(I32), 0)
         position = keep.tile([P, 1], F32)
         nc.gpsimd.iota(
             position[:], pattern=[[0, 1]], base=0, channel_multiplier=1, allow_small_or_imprecise_dtypes=True
         )
-        plane_q = keep.tile([P, Q_HEADS * HEAD_DIM], U8, align_bytes=64)
-        nc.gpsimd.memset(plane_q[:].bitcast(F32), 0.0)
         load_scales(nc, plane_q[:], wq_scales)
         wq_rest = keep.tile([P, 2 * (Q_BANKS - 1) * BANK_COLS], U8, align_bytes=64)
         nc.sync.dma_start(out=wq_rest[:].bitcast(I32), in_=wq_bytes[:, bank_words:])

import math
from contextlib import ExitStack

import concourse.mybir as mybir
from concourse.masks import make_identity

F32 = mybir.dt.float32
BF16 = mybir.dt.bfloat16
I32 = mybir.dt.int32
U32 = mybir.dt.uint32
U8 = mybir.dt.uint8
FP8X4 = mybir.dt.float8_e4m3fn_x4
FP4X4 = mybir.dt.float4_e2m1fn_x4
ALU = mybir.AluOpType
ACT = mybir.ActivationFunctionType

P = 128
TOKENS = 128
D_MODEL = 512
HEAD_DIM = 128
PAIRS = HEAD_DIM // 2
Q_HEADS = 16
KV_HEADS = 4
ROPE_THETA = 10000.0
BANK_COLS = 512
BANK_HEADS = BANK_COLS // HEAD_DIM
Q_BANKS = Q_HEADS // BANK_HEADS
N_BANKS = (Q_HEADS + 2 * KV_HEADS) // BANK_HEADS
QUADRANT = 32
LIVE_ROWS = 4
ROUND_MAGIC = 1.5 * 2.0**23
COS = 0
SIN = 1
GPSIMD_HEADS = (3, 3, 1, 0)

FLOPS = 2 * TOKENS * D_MODEL * (Q_HEADS + 2 * KV_HEADS) * HEAD_DIM


def load_words(nc, pool, words, name):
    words_sb = pool.tile([P, words.shape[2]], U8, name=name, align_bytes=64)
    nc.sync.dma_start(out=words_sb[:].bitcast(I32), in_=words.bitcast(I32)[0])
    return words_sb


def load_scales(nc, plane, scales):
    rows = scales.bitcast(I32)[0].rearrange("(q r) n -> r q n", r=LIVE_ROWS)
    for r in range(LIVE_ROWS):
        nc.sync.dma_start(out=plane.bitcast(I32)[r:P:QUADRANT, :], in_=rows[r])


def multiply_heads(multiplier, acc, table, products):
    shape = products.shape
    multiplier.tensor_tensor(
        out=products,
        in0=acc.rearrange("p (h d) -> p h d", d=shape[3]).unsqueeze(1).to_broadcast(shape),
        in1=table[:].unsqueeze(2).to_broadcast(shape),
        op=ALU.mult,
    )


def add_heads(adder, products, rotated):
    pairs = "p h (j e) -> p (h j) e"
    adder.tensor_tensor(
        out=rotated.rearrange("p (n e) -> p n e", e=2),
        in0=products[:, COS].rearrange(pairs, e=2),
        in1=products[:, SIN].rearrange(pairs, e=2)[:, :, ::-1],
        op=ALU.add,
    )


def add_heads_in_psum(nc, pool, ident, products, rotated):
    pairs = "p h (j e) -> p (h j) e"
    total = pool.tile([TOKENS, rotated.shape[1]], F32, tag="acc")
    total_pairs = total[:].rearrange("p (n e) -> p n e", e=2)
    cos_products = products[:, COS].rearrange(pairs, e=2)
    sin_products = products[:, SIN].rearrange(pairs, e=2)[:, :, ::-1]
    nc.tensor.matmul(out=total_pairs, lhsT=ident[:], rhs=cos_products, start=True, stop=False)
    nc.tensor.matmul(out=total_pairs, lhsT=ident[:], rhs=sin_products, start=False, stop=True)
    nc.scalar.copy(out=rotated, in_=total[:])


def tile_rptattention_pa_s_kernel(
    tc, hidden_states, wq_words, wq_scales, wk_words, wk_scales, wv_words, wv_scales, out_0, out_1, out_2
):
    nc = tc.nc
    with ExitStack() as ctx:
        keep = ctx.enter_context(tc.tile_pool(name="keep", bufs=1))
        work = ctx.enter_context(tc.tile_pool(name="work", bufs=N_BANKS))
        psum_x = ctx.enter_context(tc.psum_pool(name="psum_x", bufs=1))
        psum_acc = ctx.enter_context(tc.psum_pool(name="psum_acc", bufs=7))
        ctx.enter_context(tc.manual_schedule())

        x_sb = keep.tile([TOKENS, D_MODEL], BF16)
        nc.sync.dma_start(out=x_sb[:], in_=hidden_states.rearrange("b s d -> (b s) d"))
        wq_bytes = wq_words.bitcast(I32)[0]
        bank_words = 2 * BANK_COLS // 4
        wq_first = keep.tile([P, 2 * BANK_COLS], U8, align_bytes=64)
        nc.sync.dma_start(out=wq_first[:].bitcast(I32), in_=wq_bytes[:, 0:bank_words])
        plane_q = keep.tile([P, Q_HEADS * HEAD_DIM], U8, align_bytes=64)
        nc.vector.memset(plane_q[:].bitcast(I32), 0)
        position = keep.tile([P, 1], F32)
        nc.gpsimd.iota(
            position[:], pattern=[[0, 1]], base=0, channel_multiplier=1, allow_small_or_imprecise_dtypes=True
        )
        load_scales(nc, plane_q[:], wq_scales)
        wq_rest = keep.tile([P, 2 * (Q_BANKS - 1) * BANK_COLS], U8, align_bytes=64)
        nc.sync.dma_start(out=wq_rest[:].bitcast(I32), in_=wq_bytes[:, bank_words:])
        wv_sb = load_words(nc, keep, wv_words, "wv_sb")

        ident = keep.tile([P, P], F32)
        make_identity(nc, ident[:])
        warmed = keep.tile([P, 1], F32)
        nc.scalar.activation(out=warmed[:], in_=position[:], func=ACT.Sin, scale=0.0)

        plane_k = keep.tile([P, KV_HEADS * HEAD_DIM], U8, align_bytes=64)
        plane_v = keep.tile([P, KV_HEADS * HEAD_DIM], U8, align_bytes=64)
        ratio = ROPE_THETA ** (-2.0 / HEAD_DIM)
        zeros = keep.tile([P, PAIRS], F32)
        nc.vector.memset(zeros[:], 0.0)
        nc.vector.memset(plane_v[:].bitcast(I32), 0)
        ratios = keep.tile([P, PAIRS], F32)
        nc.vector.tensor_scalar_add(out=ratios[:], in0=zeros[:], scalar1=ratio)
        nc.vector.memset(plane_k[:].bitcast(I32), 0)
        load_scales(nc, plane_v[:], wv_scales)
        wk_sb = load_words(nc, keep, wk_words, "wk_sb")
        load_scales(nc, plane_k[:], wk_scales)
        start = keep.tile([P, 1], F32)
        nc.vector.tensor_scalar_mul(out=start[:], in0=position[:], scalar1=1.0 / (2.0 * math.pi * ratio))
        angle = keep.tile([P, 2, PAIRS], F32)
        nc.vector.tensor_tensor_scan(
            out=angle[:, 0, :], data0=ratios[:], data1=zeros[:], initial=start[:, 0:1], op0=ALU.mult, op1=ALU.add
        )
        nc.vector.tensor_scalar_add(out=angle[:, 1, :], in0=angle[:, 0, :], scalar1=0.25)
        whole = keep.tile([P, 2, PAIRS], F32)
        nc.vector.tensor_scalar(
            out=whole[:], in0=angle[:], scalar1=ROUND_MAGIC, scalar2=ROUND_MAGIC, op0=ALU.add, op1=ALU.subtract
        )
        part = keep.tile([P, 2, PAIRS], F32)
        nc.vector.tensor_tensor(out=part[:], in0=angle[:], in1=whole[:], op=ALU.subtract)

        x_pairs = x_sb[:].bitcast(F32)
        halves = psum_x.tile([P, 2, TOKENS], F32, tag="acc")
        for u in range(2):
            nc.tensor.transpose(out=halves[:, u, :], in_=x_pairs[:, u : D_MODEL // 2 : 2], identity=ident[:])
        grouped = keep.tile([P, 4 * TOKENS], BF16, align_bytes=64)
        x_codes = keep.tile([P, TOKENS], U32, align_bytes=64)
        x_scales = keep.tile([P, TOKENS], U8, align_bytes=64)
        for first in range(0, TOKENS, TOKENS // 2):
            tokens = slice(first, first + TOKENS // 2)
            values = grouped[:, 4 * tokens.start : 4 * tokens.stop]
            nc.scalar.copy(
                out=values.bitcast(F32).rearrange("p (r u) -> p r u", u=2),
                in_=halves[:, :, tokens].rearrange("p u r -> p r u"),
            )
            nc.vector.quantize_mx(out=x_codes[:, tokens].bitcast(FP8X4), scales=x_scales[:, tokens], in_=values)
        table = keep.tile([P, 2, HEAD_DIM], F32)
        by_pair = table[:].rearrange("p c (j e) -> p c j e", e=2)
        nc.scalar.activation(
            out=by_pair[:, COS],
            in_=part[:, 1, :].unsqueeze(2).to_broadcast([P, PAIRS, 2]),
            func=ACT.Sin,
            scale=2.0 * math.pi,
        )
        nc.scalar.activation(out=by_pair[:, SIN, :, 0], in_=part[:, 0, :], func=ACT.Sin, scale=2.0 * math.pi)
        nc.scalar.activation(out=by_pair[:, SIN, :, 1], in_=part[:, 0, :], func=ACT.Sin, scale=-2.0 * math.pi)

        def project(pool, words, plane):
            acc = pool.tile([TOKENS, plane.shape[1]], F32, tag="acc")
            nc.tensor.matmul_mx(
                out=acc[:],
                lhsT=x_codes[:].bitcast(FP8X4),
                lhsT_scale=x_scales[:],
                rhs=words.bitcast(FP4X4),
                rhs_scale=plane,
                start=True,
                stop=True,
            )
            return acc

        flat = "b s h d -> (b s) (h d)"
        q_rot = out_0.rearrange(flat)

        def q_bank(b):
            cols = slice(b * BANK_COLS, (b + 1) * BANK_COLS)
            words = wq_first[:] if b == 0 else wq_rest[:, 2 * (b - 1) * BANK_COLS : 2 * b * BANK_COLS]
            return words, plane_q[:, cols], q_rot[:, cols]

        def head_cols(first, stop):
            return slice(first * HEAD_DIM, stop * HEAD_DIM)

        def first_pass(first, count):
            words, plane, dest = q_bank(0)
            cols = head_cols(first, first + count)
            return project(psum_acc, words[:, 2 * cols.start : 2 * cols.stop], plane[:, cols])

        acc_0 = first_pass(0, 1)
        acc_12 = first_pass(1, 2)
        acc_3 = first_pass(3, 1)
        own = keep.tile([TOKENS, HEAD_DIM], F32)
        nc.scalar.copy(out=own[:], in_=acc_3[:])
        accs = []
        for b in range(1, Q_BANKS):
            words, plane, dest = q_bank(b)
            accs.append(project(psum_acc, words, plane))
        acc_v = project(psum_x, wv_sb[:], plane_v[:])
        v_sb = keep.tile([TOKENS, BANK_COLS], F32)
        nc.scalar.copy(out=v_sb[:], in_=acc_v[:])
        nc.sync.dma_start(out=out_2.rearrange(flat), in_=v_sb[:])

        own_products = work.tile([TOKENS, 2, 1, HEAD_DIM], F32, name="own_products")
        multiply_heads(nc.gpsimd, own[:], table, own_products[:])
        products_0 = work.tile([TOKENS, 2, 1, HEAD_DIM], F32, name="products_0")
        multiply_heads(nc.vector, acc_0[:], table, products_0[:])
        products_12 = work.tile([TOKENS, 2, 2, HEAD_DIM], F32, name="products_12")
        multiply_heads(nc.vector, acc_12[:], table, products_12[:])
        rotated = work.tile([TOKENS, BANK_COLS], F32)
        add_heads_in_psum(nc, psum_acc, ident, products_0[:], rotated[:, head_cols(0, 1)])
        add_heads(nc.gpsimd, products_12[:], rotated[:, head_cols(1, 3)])
        add_heads(nc.gpsimd, own_products[:], rotated[:, head_cols(3, 4)])
        nc.sync.dma_start(out=q_bank(0)[2], in_=rotated[:])

        accs.append(project(psum_acc, wk_sb[:], plane_k[:]))
        dests = [q_bank(b)[2] for b in range(1, Q_BANKS)] + [out_1.rearrange(flat)]
        waiting = []
        for acc, by_gpsimd, dest in zip(accs, GPSIMD_HEADS, dests):
            products = work.tile([TOKENS, 2, BANK_HEADS, HEAD_DIM], F32, name="products")
            multiply_heads(nc.vector, acc[:], table, products[:])
            rotated = work.tile([TOKENS, BANK_COLS], F32)
            left = 0
            if by_gpsimd:
                add_heads(nc.gpsimd, products[:, :, :by_gpsimd], rotated[:, head_cols(0, by_gpsimd)])
                left = by_gpsimd + 1
                add_heads_in_psum(nc, psum_acc, ident, products[:, :, by_gpsimd:left], rotated[:, head_cols(by_gpsimd, left)])
            if left < BANK_HEADS:
                waiting.append((products, left, rotated, dest))
            else:
                nc.sync.dma_start(out=dest, in_=rotated[:])
        for products, left, rotated, dest in waiting:
            add_heads(nc.vector, products[:, :, left:], rotated[:, head_cols(left, BANK_HEADS)])
            nc.sync.dma_start(out=dest, in_=rotated[:])
